import numpy as np
import ml_dtypes


def mxq(x, axis, fmt="e4m3"):
    dtype, down = {"e4m3": (ml_dtypes.float8_e4m3fn, 7), "e5m2": (ml_dtypes.float8_e5m2, 14)}[fmt]
    v = np.moveaxis(np.asarray(x, np.float32).astype(ml_dtypes.bfloat16).astype(np.float64), axis, -1)
    blocks = v.reshape(v.shape[:-1] + (-1, 32))
    amax = np.abs(blocks).max(-1, keepdims=True)
    byte = np.maximum(np.where(amax > 0, np.frexp(amax)[1] - 1 + 127, 0) - down, 1)
    scale = np.exp2(byte - 127.0)
    codes = (blocks / scale).astype(np.float32).astype(dtype).astype(np.float64)
    return np.moveaxis((codes * scale).reshape(v.shape), -1, axis)


WIDE = False


def mx_kscale(k):
    if not WIDE:
        return np.ones(k)
    levels = np.array([10, -10, 5, -5, 0])
    a = np.random.permutation(np.resize(levels, k // 512 * 4)).reshape(k // 512, 4)
    idx = np.arange(k)
    return np.exp2(a[idx // 512, idx % 128 // 32])


BF16 = ml_dtypes.bfloat16


def bf(x):
    return np.asarray(x, np.float32).astype(BF16)


def f64(x):
    return np.asarray(x).astype(np.float64)


E2M1 = np.array([0.0, 0.5, 1.0, 1.5, 2.0, 3.0, 4.0, 6.0, -0.0, -0.5, -1.0, -1.5, -2.0, -3.0, -4.0, -6.0])


def pack_weight(w, fmt):
    k, n = w.shape
    w = f64(bf(w)).reshape(k // 32, 32, n)
    amax = np.abs(w).max(1)
    if fmt == "e4m3":
        byte = np.frexp(amax)[1] - 1 + 127 - 7
    else:
        mant, ex = np.frexp(amax / 6.0)
        byte = np.where(mant > 0.5, ex, ex - 1) + 127
    byte = np.clip(np.where(amax > 0, byte, 1), 1, 254)
    scaled = (w * np.exp2(127.0 - byte)[:, None, :]).reshape(k, n).astype(np.float32)
    by_word = np.ascontiguousarray(scaled.reshape(k // 512, 128, 4, n).transpose(0, 1, 3, 2))
    if fmt == "e4m3":
        words = by_word.astype(ml_dtypes.float8_e4m3fn).view(np.uint8)
    else:
        c = by_word.astype(ml_dtypes.float4_e2m1fn).view(np.uint8) & 0xF
        words = c[..., 0::2] | (c[..., 1::2] << 4)
    return np.ascontiguousarray(words), np.ascontiguousarray(byte.astype(np.uint8).reshape(k // 512, 16, n))


def unpack_weight(words, scales, fmt):
    g, p, n, _ = words.shape
    if fmt == "e4m3":
        vals = np.ascontiguousarray(words).view(ml_dtypes.float8_e4m3fn).astype(np.float64)
    else:
        nib = np.empty((g, p, n, 4), np.uint8)
        nib[..., 0::2] = words & 0xF
        nib[..., 1::2] = words >> 4
        vals = E2M1[nib]
    vals = vals * np.repeat(np.exp2(scales.astype(np.float64) - 127.0), 8, axis=1)[..., None]
    return vals.transpose(0, 1, 3, 2).reshape(g * 512, n)


S, B, SC = 1024, 1024, 4096


def setup_inputs():
    s = mx_kscale(B)
    proba = bf((np.random.standard_normal((S, B)) * s).reshape(-1))
    cur_inven = bf(np.random.random_sample((S, SC)))
    words, scales = pack_weight(np.random.random_sample((B, SC)) * (16.0 / np.sqrt(B)) / s[:, None], "e4m3")
    avail_bundle = bf(np.random.random_sample(B) * s)
    alloc_bundle = bf(np.random.random_sample(B) * s)
    return {"proba": proba,
            "cur_inven": cur_inven,
            "bun_sc_words": words,
            "bun_sc_scales": scales,
            "avail_bundle": avail_bundle,
            "alloc_bundle": alloc_bundle}


def reference(proba, cur_inven, bun_sc_words, bun_sc_scales, avail_bundle, alloc_bundle):
    p = f64(proba).reshape(S, B)
    av = f64(avail_bundle)
    al = f64(alloc_bundle)
    over_avail = (av[None, :] - p < 0.0) & (p > 0.0)
    over_alloc = (al[None, :] + p < 0.0) & (p < 0.0)
    cm = np.where(over_avail | over_alloc, 0.01, 1.0)
    next_inven = f64(cur_inven) + (mxq(p * cm, 1, "e4m3") @ unpack_weight(bun_sc_words, bun_sc_scales, "e4m3"))
    return next_inven.reshape(1, -1)

@@ -1,0 +1,170 @@
+import concourse.mybir as mybir
+from concourse.masks import make_identity
+
+F32 = mybir.dt.float32
+BF16 = mybir.dt.bfloat16
+I32 = mybir.dt.int32
+U32 = mybir.dt.uint32
+U8 = mybir.dt.uint8
+FP8X4 = mybir.dt.float8_e4m3fn_x4
+ALU = mybir.AluOpType
+
+P = 128
+PACK = 4
+K_PASS = P * PACK
+SHOPS = 1024
+BUNDLES = 1024
+COLS = 4096
+GROUPS = BUNDLES // K_PASS
+M_TILES = SHOPS // P
+N_TILE = 512
+N_TILES = COLS // N_TILE
+HALVES = 2
+HALF_TILES = M_TILES // HALVES
+HALF_SHOPS = HALF_TILES * P
+QUADRANTS = 4
+PLANE_COLS = COLS // 4
+DAMPING = 0.01
+
+FLOPS = 2 * SHOPS * BUNDLES * COLS
+
+
+def tile_optblockv2_kernel(
+    tc, proba, cur_inven, bun_sc_words, bun_sc_scales, avail_bundle, alloc_bundle, out
+):
+    nc = tc.nc
+    p_view = proba.rearrange("(r m k) -> r m k", m=M_TILES, k=BUNDLES)
+    cur_view = cur_inven.rearrange("(r m) n -> r m n", m=M_TILES)
+    out_view = out.rearrange("o (r m n) -> (o r) m n", m=M_TILES, n=COLS)
+
+    with tc.tile_pool(name="keep", bufs=1) as keep:
+        w_words = keep.tile([P, GROUPS, COLS], U32, align_bytes=64)
+        w_planes = keep.tile([P, GROUPS, PLANE_COLS], U8, align_bytes=64)
+        cur_sb = keep.tile([P, M_TILES, COLS], BF16)
+        h_words = keep.tile([P, HALVES, GROUPS, HALF_SHOPS], U32, align_bytes=64)
+        h_planes = keep.tile([P, HALVES, GROUPS, HALF_SHOPS], U8, align_bytes=64)
+        identity = keep.tile([P, P], BF16)
+        avail_sb = keep.tile([P, GROUPS * PACK], BF16)
+        alloc_sb = keep.tile([P, GROUPS * PACK], BF16)
+        upper = keep.tile([P, GROUPS * PACK], F32)
+        lower = keep.tile([P, GROUPS * PACK], F32)
+
+        nc.vector.memset(w_planes[:].bitcast(I32), 0)
+        make_identity(nc, identity[:])
+
+        with (
+            tc.tile_pool(name="front", bufs=1) as front,
+            tc.tile_pool(name="work", bufs=2) as work,
+            tc.psum_pool(name="flip", bufs=4) as flip,
+        ):
+            p_sb = front.tile([P, M_TILES, BUNDLES], BF16)
+            p_flipped = front.tile([P, HALVES, GROUPS, PACK, HALF_SHOPS], BF16)
+
+            nc.scalar.dma_start(
+                out=avail_sb[:].rearrange("q (g t) -> q g t", t=PACK),
+                in_=avail_bundle.rearrange("(g q t) -> q g t", g=GROUPS, t=PACK),
+            )
+            nc.scalar.dma_start(
+                out=alloc_sb[:].rearrange("q (g t) -> q g t", t=PACK),
+                in_=alloc_bundle.rearrange("(g q t) -> q g t", g=GROUPS, t=PACK),
+            )
+            for a in range(HALVES):
+                tiles = slice(a * HALF_TILES, (a + 1) * HALF_TILES)
+                nc.sync.dma_start(out=p_sb[:, tiles, :], in_=p_view[:, tiles, :])
+            for g in range(GROUPS):
+                for quadrant in range(QUADRANTS):
+                    rows = bun_sc_scales[g, 4 * quadrant : 4 * quadrant + 4, :].bitcast(I32)
+                    nc.sync.dma_start(
+                        out=w_planes[32 * quadrant : 32 * quadrant + 16, g, :].bitcast(I32),
+                        in_=rows.rearrange("r (j n) -> j r n", j=4),
+                    )
+            for c in range(2):
+                for g in range(GROUPS):
+                    cols = slice(c * (COLS // 2), (c + 1) * (COLS // 2))
+                    packed = bun_sc_words[g].rearrange("q n t -> q (n t)").bitcast(I32)
+                    nc.sync.dma_start(out=w_words[:, g, cols].bitcast(I32), in_=packed[:, cols])
+            for m in range(0, M_TILES, 2):
+                nc.sync.dma_start(out=cur_sb[:, m : m + 2, :], in_=cur_view[:, m : m + 2, :])
+
+            nc.vector.tensor_scalar_max(out=upper[:], in0=avail_sb[:], scalar1=0.0)
+            nc.vector.tensor_scalar(
+                out=lower[:], in0=alloc_sb[:], scalar1=-1.0, scalar2=0.0, op0=ALU.mult, op1=ALU.min
+            )
+
+            for a in range(HALVES):
+                for g in range(GROUPS):
+                    for t in range(PACK):
+                        flipped_ps = flip.tile([P, HALF_SHOPS], BF16)
+                        for i in range(HALF_TILES):
+                            nc.tensor.transpose(
+                                out=flipped_ps[:, i * P : (i + 1) * P],
+                                in_=p_sb[:, a * HALF_TILES + i, K_PASS * g + t : K_PASS * (g + 1) : PACK],
+                                identity=identity[:],
+                            )
+                        nc.scalar.copy(out=p_flipped[:, a, g, t, :], in_=flipped_ps[:])
+
+            def damp(a, g):
+                p_part = p_flipped[:, a, g]
+                clamped = work.tile([P, PACK, HALF_SHOPS], BF16)
+                for t in range(PACK):
+                    column = slice(g * PACK + t, g * PACK + t + 1)
+                    nc.vector.tensor_scalar(
+                        out=clamped[:, t, :],
+                        in0=p_part[:, t, :],
+                        scalar1=lower[:, column],
+                        scalar2=upper[:, column],
+                        op0=ALU.max,
+                        op1=ALU.min,
+                    )
+                inside = work.tile([P, PACK, HALF_SHOPS], BF16)
+                nc.vector.tensor_tensor(out=inside[:], in0=clamped[:], in1=p_part, op=ALU.is_equal)
+                damped = work.tile([P, PACK, HALF_SHOPS], BF16)
+                nc.vector.scalar_tensor_tensor(
+                    out=damped[:], in0=inside[:], scalar=DAMPING, in1=p_part, op0=ALU.max, op1=ALU.mult
+                )
+                grouped = work.tile([P, HALF_SHOPS, PACK], BF16, align_bytes=64)
+                nc.scalar.copy(out=grouped[:], in_=damped[:].rearrange("q t s -> q s t"))
+                return grouped
+
+            def quantise(a, g, grouped):
+                nc.vector.quantize_mx(
+                    out=h_words[:, a, g, :].bitcast(FP8X4),
+                    scales=h_planes[:, a, g, :],
+                    in_=grouped[:].rearrange("q s t -> q (s t)"),
+                )
+
+            parts = [(a, g) for a in range(HALVES) for g in range(GROUPS)]
+            waiting = None
+            for a, g in parts:
+                grouped = damp(a, g)
+                if waiting is not None:
+                    quantise(*waiting)
+                waiting = (a, g, grouped)
+            quantise(*waiting)
+
+        with (
+            tc.tile_pool(name="results", bufs=4) as results,
+            tc.psum_pool(name="sums", bufs=8) as sums,
+        ):
+            for m in range(M_TILES):
+                a, i = divmod(m, HALF_TILES)
+                shops = slice(i * P, (i + 1) * P)
+                result = results.tile([P, COLS], F32)
+                for n in range(N_TILES):
+                    cols = slice(n * N_TILE, (n + 1) * N_TILE)
+                    j, part = divmod(n * N_TILE, PLANE_COLS)
+                    acc = sums.tile([P, N_TILE], F32)
+                    for g in range(GROUPS):
+                        nc.tensor.matmul_mx(
+                            out=acc[:],
+                            lhsT=h_words[:, a, g, shops].bitcast(FP8X4),
+                            lhsT_scale=h_planes[:, a, g, shops],
+                            rhs=w_words[:, g, cols].bitcast(FP8X4),
+                            rhs_scale=w_planes[4 * j : P, g, part : part + N_TILE],
+                            start=(g == 0),
+                            stop=(g == GROUPS - 1),
+                        )
+                    nc.vector.tensor_tensor(
+                        out=result[:, cols], in0=acc[:], in1=cur_sb[:, m, cols], op=ALU.add
+                    )
+                nc.sync.dma_start(out=out_view[:, m, :], in_=result[:])

@@ -25,6 +25,7 @@ HALF_SHOPS = HALF_TILES * P
 QUADRANTS = 4
 PLANE_COLS = COLS // 4
 DAMPING = 0.01
+RELIEF_EVERY = 4
 
 FLOPS = 2 * SHOPS * BUNDLES * COLS
 
@@ -164,7 +165,13 @@ def tile_optblockv2_kernel(
                             start=(g == 0),
                             stop=(g == GROUPS - 1),
                         )
-                    nc.vector.tensor_tensor(
-                        out=result[:, cols], in0=acc[:], in1=cur_sb[:, m, cols], op=ALU.add
-                    )
+                    if n % RELIEF_EVERY == 1:
+                        nc.scalar.copy(out=result[:, cols], in_=acc[:])
+                        nc.gpsimd.tensor_tensor(
+                            out=result[:, cols], in0=result[:, cols], in1=cur_sb[:, m, cols], op=ALU.add
+                        )
+                    else:
+                        nc.vector.tensor_tensor(
+                            out=result[:, cols], in0=acc[:], in1=cur_sb[:, m, cols], op=ALU.add
+                        )
                 nc.sync.dma_start(out=out_view[:, m, :], in_=result[:])

@@ -22,10 +22,10 @@ N_TILES = COLS // N_TILE
 HALVES = 2
 HALF_TILES = M_TILES // HALVES
 HALF_SHOPS = HALF_TILES * P
-QUADRANTS = 4
 PLANE_COLS = COLS // 4
 DAMPING = 0.01
 RELIEF_EVERY = 4
+LAST_STORES = 4
 
 FLOPS = 2 * SHOPS * BUNDLES * COLS
 
@@ -38,140 +38,144 @@ def tile_optblockv2_kernel(
     cur_view = cur_inven.rearrange("(r m) n -> r m n", m=M_TILES)
     out_view = out.rearrange("o (r m n) -> (o r) m n", m=M_TILES, n=COLS)
 
-    with tc.tile_pool(name="keep", bufs=1) as keep:
+    with (
+        tc.tile_pool(name="keep", bufs=1) as keep,
+        tc.tile_pool(name="work", bufs=2) as work,
+        tc.tile_pool(name="results", bufs=4) as results,
+        tc.psum_pool(name="flip", bufs=2) as flip,
+        tc.psum_pool(name="sums", bufs=6) as sums,
+    ):
+        p_sb = keep.tile([P, M_TILES, BUNDLES], BF16)
         w_words = keep.tile([P, GROUPS, COLS], U32, align_bytes=64)
         w_planes = keep.tile([P, GROUPS, PLANE_COLS], U8, align_bytes=64)
         cur_sb = keep.tile([P, M_TILES, COLS], BF16)
-        h_words = keep.tile([P, HALVES, GROUPS, HALF_SHOPS], U32, align_bytes=64)
-        h_planes = keep.tile([P, HALVES, GROUPS, HALF_SHOPS], U8, align_bytes=64)
-        identity = keep.tile([P, P], BF16)
         avail_sb = keep.tile([P, GROUPS * PACK], BF16)
         alloc_sb = keep.tile([P, GROUPS * PACK], BF16)
         upper = keep.tile([P, GROUPS * PACK], F32)
         lower = keep.tile([P, GROUPS * PACK], F32)
+        identity = keep.tile([P, P], BF16)
+        p_flipped = keep.tile([P, HALVES, GROUPS, PACK, HALF_SHOPS], BF16)
+        h_words = keep.tile([P, HALVES, GROUPS, HALF_SHOPS], U32, align_bytes=64)
+        h_planes = keep.tile([P, HALVES, GROUPS, HALF_SHOPS], U8, align_bytes=64)
 
         nc.vector.memset(w_planes[:].bitcast(I32), 0)
         make_identity(nc, identity[:])
 
-        with (
-            tc.tile_pool(name="front", bufs=1) as front,
-            tc.tile_pool(name="work", bufs=2) as work,
-            tc.psum_pool(name="flip", bufs=4) as flip,
-        ):
-            p_sb = front.tile([P, M_TILES, BUNDLES], BF16)
-            p_flipped = front.tile([P, HALVES, GROUPS, PACK, HALF_SHOPS], BF16)
+        nc.scalar.dma_start(
+            out=avail_sb[:].rearrange("q (g t) -> q g t", t=PACK),
+            in_=avail_bundle.rearrange("(g q t) -> q g t", g=GROUPS, t=PACK),
+        )
+        nc.scalar.dma_start(
+            out=alloc_sb[:].rearrange("q (g t) -> q g t", t=PACK),
+            in_=alloc_bundle.rearrange("(g q t) -> q g t", g=GROUPS, t=PACK),
+        )
 
-            nc.scalar.dma_start(
-                out=avail_sb[:].rearrange("q (g t) -> q g t", t=PACK),
-                in_=avail_bundle.rearrange("(g q t) -> q g t", g=GROUPS, t=PACK),
-            )
-            nc.scalar.dma_start(
-                out=alloc_sb[:].rearrange("q (g t) -> q g t", t=PACK),
-                in_=alloc_bundle.rearrange("(g q t) -> q g t", g=GROUPS, t=PACK),
-            )
-            for a in range(HALVES):
-                tiles = slice(a * HALF_TILES, (a + 1) * HALF_TILES)
-                nc.sync.dma_start(out=p_sb[:, tiles, :], in_=p_view[:, tiles, :])
+        def load_p(a):
+            tiles = slice(a * HALF_TILES, (a + 1) * HALF_TILES)
+            nc.sync.dma_start(out=p_sb[:, tiles, :], in_=p_view[:, tiles, :])
+
+        def load_w_words(g):
+            packed = bun_sc_words[g].rearrange("q n t -> q (n t)").bitcast(I32)
+            nc.sync.dma_start(out=w_words[:, g, :].bitcast(I32), in_=packed)
+
+        def load_w_scales(g, quadrants):
+            for quadrant in quadrants:
+                rows = bun_sc_scales[g, 4 * quadrant : 4 * quadrant + 4, :].bitcast(I32)
+                nc.sync.dma_start(
+                    out=w_planes[32 * quadrant : 32 * quadrant + 16, g, :].bitcast(I32),
+                    in_=rows.rearrange("r (j n) -> j r n", j=4),
+                )
+
+        load_p(0)
+        load_w_scales(0, (0, 1))
+        load_p(1)
+        load_w_scales(0, (2, 3))
+        load_w_words(0)
+        load_w_scales(1, (0, 1))
+        load_w_words(1)
+        load_w_scales(1, (2, 3))
+        for m in range(0, M_TILES, 2):
+            nc.sync.dma_start(out=cur_sb[:, m : m + 2, :], in_=cur_view[:, m : m + 2, :])
+
+        nc.vector.tensor_scalar_max(out=upper[:], in0=avail_sb[:], scalar1=0.0)
+        nc.vector.tensor_scalar(
+            out=lower[:], in0=alloc_sb[:], scalar1=-1.0, scalar2=0.0, op0=ALU.mult, op1=ALU.min
+        )
+
+        for a in range(HALVES):
             for g in range(GROUPS):
-                for quadrant in range(QUADRANTS):
-                    rows = bun_sc_scales[g, 4 * quadrant : 4 * quadrant + 4, :].bitcast(I32)
-                    nc.sync.dma_start(
-                        out=w_planes[32 * quadrant : 32 * quadrant + 16, g, :].bitcast(I32),
-                        in_=rows.rearrange("r (j n) -> j r n", j=4),
-                    )
-            for c in range(2):
-                for g in range(GROUPS):
-                    cols = slice(c * (COLS // 2), (c + 1) * (COLS // 2))
-                    packed = bun_sc_words[g].rearrange("q n t -> q (n t)").bitcast(I32)
-                    nc.sync.dma_start(out=w_words[:, g, cols].bitcast(I32), in_=packed[:, cols])
-            for m in range(0, M_TILES, 2):
-                nc.sync.dma_start(out=cur_sb[:, m : m + 2, :], in_=cur_view[:, m : m + 2, :])
+                for t in range(PACK):
+                    flipped_ps = flip.tile([P, HALF_SHOPS], BF16)
+                    for i in range(HALF_TILES):
+                        nc.tensor.transpose(
+                            out=flipped_ps[:, i * P : (i + 1) * P],
+                            in_=p_sb[:, a * HALF_TILES + i, K_PASS * g + t : K_PASS * (g + 1) : PACK],
+                            identity=identity[:],
+                        )
+                    nc.scalar.copy(out=p_flipped[:, a, g, t, :], in_=flipped_ps[:])
 
-            nc.vector.tensor_scalar_max(out=upper[:], in0=avail_sb[:], scalar1=0.0)
-            nc.vector.tensor_scalar(
-                out=lower[:], in0=alloc_sb[:], scalar1=-1.0, scalar2=0.0, op0=ALU.mult, op1=ALU.min
+        def prepare_h(a, g):
+            p_part = p_flipped[:, a, g]
+            clamped = work.tile([P, PACK, HALF_SHOPS], BF16, bufs=1)
+            for t in range(PACK):
+                column = slice(g * PACK + t, g * PACK + t + 1)
+                nc.vector.tensor_scalar(
+                    out=clamped[:, t, :],
+                    in0=p_part[:, t, :],
+                    scalar1=lower[:, column],
+                    scalar2=upper[:, column],
+                    op0=ALU.max,
+                    op1=ALU.min,
+                )
+            inside = work.tile([P, PACK, HALF_SHOPS], BF16, bufs=1)
+            nc.vector.tensor_tensor(out=inside[:], in0=clamped[:], in1=p_part, op=ALU.is_equal)
+            damped = work.tile([P, PACK, HALF_SHOPS], BF16)
+            nc.vector.scalar_tensor_tensor(
+                out=damped[:], in0=inside[:], scalar=DAMPING, in1=p_part, op0=ALU.max, op1=ALU.mult
+            )
+            grouped = work.tile([P, HALF_SHOPS, PACK], BF16, align_bytes=64)
+            nc.scalar.copy(out=grouped[:], in_=damped[:].rearrange("q t s -> q s t"))
+            nc.vector.quantize_mx(
+                out=h_words[:, a, g, :].bitcast(FP8X4),
+                scales=h_planes[:, a, g, :],
+                in_=grouped[:].rearrange("q s t -> q (s t)"),
             )
 
-            for a in range(HALVES):
+        def shop_tile(m):
+            a, i = divmod(m, HALF_TILES)
+            shops = slice(i * P, (i + 1) * P)
+            result = results.tile([P, COLS], F32)
+            for n in range(N_TILES):
+                cols = slice(n * N_TILE, (n + 1) * N_TILE)
+                j, part = divmod(n * N_TILE, PLANE_COLS)
+                acc = sums.tile([P, N_TILE], F32)
                 for g in range(GROUPS):
-                    for t in range(PACK):
-                        flipped_ps = flip.tile([P, HALF_SHOPS], BF16)
-                        for i in range(HALF_TILES):
-                            nc.tensor.transpose(
-                                out=flipped_ps[:, i * P : (i + 1) * P],
-                                in_=p_sb[:, a * HALF_TILES + i, K_PASS * g + t : K_PASS * (g + 1) : PACK],
-                                identity=identity[:],
-                            )
-                        nc.scalar.copy(out=p_flipped[:, a, g, t, :], in_=flipped_ps[:])
-
-            def damp(a, g):
-                p_part = p_flipped[:, a, g]
-                clamped = work.tile([P, PACK, HALF_SHOPS], BF16)
-                for t in range(PACK):
-                    column = slice(g * PACK + t, g * PACK + t + 1)
-                    nc.vector.tensor_scalar(
-                        out=clamped[:, t, :],
-                        in0=p_part[:, t, :],
-                        scalar1=lower[:, column],
-                        scalar2=upper[:, column],
-                        op0=ALU.max,
-                        op1=ALU.min,
+                    nc.tensor.matmul_mx(
+                        out=acc[:],
+                        lhsT=h_words[:, a, g, shops].bitcast(FP8X4),
+                        lhsT_scale=h_planes[:, a, g, shops],
+                        rhs=w_words[:, g, cols].bitcast(FP8X4),
+                        rhs_scale=w_planes[4 * j : P, g, part : part + N_TILE],
+                        start=(g == 0),
+                        stop=(g == GROUPS - 1),
                     )
-                inside = work.tile([P, PACK, HALF_SHOPS], BF16)
-                nc.vector.tensor_tensor(out=inside[:], in0=clamped[:], in1=p_part, op=ALU.is_equal)
-                damped = work.tile([P, PACK, HALF_SHOPS], BF16)
-                nc.vector.scalar_tensor_tensor(
-                    out=damped[:], in0=inside[:], scalar=DAMPING, in1=p_part, op0=ALU.max, op1=ALU.mult
-                )
-                grouped = work.tile([P, HALF_SHOPS, PACK], BF16, align_bytes=64)
-                nc.scalar.copy(out=grouped[:], in_=damped[:].rearrange("q t s -> q s t"))
-                return grouped
+                if n % RELIEF_EVERY == 1:
+                    nc.scalar.copy(out=result[:, cols], in_=acc[:])
+                    nc.gpsimd.tensor_tensor(
+                        out=result[:, cols], in0=result[:, cols], in1=cur_sb[:, m, cols], op=ALU.add
+                    )
+                else:
+                    nc.vector.tensor_tensor(
+                        out=result[:, cols], in0=acc[:], in1=cur_sb[:, m, cols], op=ALU.add
+                    )
+            stores = LAST_STORES if m == M_TILES - 1 else 1
+            for piece in range(stores):
+                cols = slice(piece * COLS // stores, (piece + 1) * COLS // stores)
+                nc.sync.dma_start(out=out_view[:, m, cols], in_=result[:, cols])
 
-            def quantise(a, g, grouped):
-                nc.vector.quantize_mx(
-                    out=h_words[:, a, g, :].bitcast(FP8X4),
-                    scales=h_planes[:, a, g, :],
-                    in_=grouped[:].rearrange("q s t -> q (s t)"),
-                )
-
-            parts = [(a, g) for a in range(HALVES) for g in range(GROUPS)]
-            waiting = None
-            for a, g in parts:
-                grouped = damp(a, g)
-                if waiting is not None:
-                    quantise(*waiting)
-                waiting = (a, g, grouped)
-            quantise(*waiting)
-
-        with (
-            tc.tile_pool(name="results", bufs=4) as results,
-            tc.psum_pool(name="sums", bufs=8) as sums,
-        ):
-            for m in range(M_TILES):
-                a, i = divmod(m, HALF_TILES)
-                shops = slice(i * P, (i + 1) * P)
-                result = results.tile([P, COLS], F32)
-                for n in range(N_TILES):
-                    cols = slice(n * N_TILE, (n + 1) * N_TILE)
-                    j, part = divmod(n * N_TILE, PLANE_COLS)
-                    acc = sums.tile([P, N_TILE], F32)
-                    for g in range(GROUPS):
-                        nc.tensor.matmul_mx(
-                            out=acc[:],
-                            lhsT=h_words[:, a, g, shops].bitcast(FP8X4),
-                            lhsT_scale=h_planes[:, a, g, shops],
-                            rhs=w_words[:, g, cols].bitcast(FP8X4),
-                            rhs_scale=w_planes[4 * j : P, g, part : part + N_TILE],
-                            start=(g == 0),
-                            stop=(g == GROUPS - 1),
-                        )
-                    if n % RELIEF_EVERY == 1:
-                        nc.scalar.copy(out=result[:, cols], in_=acc[:])
-                        nc.gpsimd.tensor_tensor(
-                            out=result[:, cols], in0=result[:, cols], in1=cur_sb[:, m, cols], op=ALU.add
-                        )
-                    else:
-                        nc.vector.tensor_tensor(
-                            out=result[:, cols], in0=acc[:], in1=cur_sb[:, m, cols], op=ALU.add
-                        )
-                nc.sync.dma_start(out=out_view[:, m, :], in_=result[:])
+        for g in range(GROUPS):
+            prepare_h(0, g)
+        for m in range(M_TILES):
+            shop_tile(m)
+            if m < GROUPS:
+                prepare_h(1, m)

@@ -19,9 +19,11 @@ GROUPS = BUNDLES // K_PASS
 M_TILES = SHOPS // P
 N_TILE = 512
 N_TILES = COLS // N_TILE
-HALVES = 2
-HALF_TILES = M_TILES // HALVES
-HALF_SHOPS = HALF_TILES * P
+PAIR_TILES = 2
+PAIRS = M_TILES // PAIR_TILES
+PAIR_SHOPS = PAIR_TILES * P
+W_PARTS = 2
+W_PART_COLS = COLS // W_PARTS
 PLANE_COLS = COLS // 4
 DAMPING = 0.01
 RELIEF_EVERY = 4
@@ -37,16 +39,18 @@ def tile_optblockv2_kernel(
     p_view = proba.rearrange("(r m k) -> r m k", m=M_TILES, k=BUNDLES)
     cur_view = cur_inven.rearrange("(r m) n -> r m n", m=M_TILES)
     out_view = out.rearrange("o (r m n) -> (o r) m n", m=M_TILES, n=COLS)
+    w_view = bun_sc_words.rearrange("g q n t -> q g (n t)")
 
     with (
         tc.tile_pool(name="keep", bufs=1) as keep,
         tc.tile_pool(name="work", bufs=2) as work,
-        tc.tile_pool(name="results", bufs=4) as results,
-        tc.psum_pool(name="flip", bufs=2) as flip,
-        tc.psum_pool(name="sums", bufs=6) as sums,
+        tc.tile_pool(name="rows", bufs=5) as rows,
+        tc.psum_pool(name="banks", bufs=8) as banks,
     ):
-        p_sb = keep.tile([P, M_TILES, BUNDLES], BF16)
-        w_words = keep.tile([P, GROUPS, COLS], U32, align_bytes=64)
+        p_sb = rows.tile([P, M_TILES, BUNDLES], BF16, tag="row")
+        w_words_a = keep.tile([P, GROUPS, W_PART_COLS], U32, align_bytes=64)
+        w_words_b = keep.tile([P, GROUPS, W_PART_COLS], U32, align_bytes=64)
+        w_words = [w_words_a, w_words_b]
         w_planes = keep.tile([P, GROUPS, PLANE_COLS], U8, align_bytes=64)
         cur_sb = keep.tile([P, M_TILES, COLS], BF16)
         avail_sb = keep.tile([P, GROUPS * PACK], BF16)
@@ -54,9 +58,9 @@ def tile_optblockv2_kernel(
         upper = keep.tile([P, GROUPS * PACK], F32)
         lower = keep.tile([P, GROUPS * PACK], F32)
         identity = keep.tile([P, P], BF16)
-        p_flipped = keep.tile([P, HALVES, GROUPS, PACK, HALF_SHOPS], BF16)
-        h_words = keep.tile([P, HALVES, GROUPS, HALF_SHOPS], U32, align_bytes=64)
-        h_planes = keep.tile([P, HALVES, GROUPS, HALF_SHOPS], U8, align_bytes=64)
+        p_flipped = keep.tile([P, PAIRS, GROUPS, PACK, PAIR_SHOPS], BF16)
+        h_words = keep.tile([P, PAIRS, GROUPS, PAIR_SHOPS], U32, align_bytes=64)
+        h_planes = keep.tile([P, PAIRS, GROUPS, PAIR_SHOPS], U8, align_bytes=64)
 
         nc.vector.memset(w_planes[:].bitcast(I32), 0)
         make_identity(nc, identity[:])
@@ -70,92 +74,126 @@ def tile_optblockv2_kernel(
             in_=alloc_bundle.rearrange("(g q t) -> q g t", g=GROUPS, t=PACK),
         )
 
-        def load_p(a):
-            tiles = slice(a * HALF_TILES, (a + 1) * HALF_TILES)
+        def load_p(first, count):
+            tiles = slice(first, first + count)
             nc.sync.dma_start(out=p_sb[:, tiles, :], in_=p_view[:, tiles, :])
 
-        def load_w_words(g):
-            packed = bun_sc_words[g].rearrange("q n t -> q (n t)").bitcast(I32)
-            nc.sync.dma_start(out=w_words[:, g, :].bitcast(I32), in_=packed)
+        def load_w_words(part):
+            packed = w_view[:, :, part * W_PART_COLS * PACK : (part + 1) * W_PART_COLS * PACK]
+            nc.sync.dma_start(out=w_words[part][:].bitcast(I32), in_=packed.bitcast(I32))
 
         def load_w_scales(g, quadrants):
             for quadrant in quadrants:
-                rows = bun_sc_scales[g, 4 * quadrant : 4 * quadrant + 4, :].bitcast(I32)
+                scale_rows = bun_sc_scales[g, 4 * quadrant : 4 * quadrant + 4, :].bitcast(I32)
                 nc.sync.dma_start(
                     out=w_planes[32 * quadrant : 32 * quadrant + 16, g, :].bitcast(I32),
-                    in_=rows.rearrange("r (j n) -> j r n", j=4),
+                    in_=scale_rows.rearrange("r (j n) -> j r n", j=4),
                 )
 
-        load_p(0)
+        def load_cur(first, count):
+            tiles = slice(first, first + count)
+            nc.sync.dma_start(out=cur_sb[:, tiles, :], in_=cur_view[:, tiles, :])
+
+        load_p(0, 4)
         load_w_scales(0, (0, 1))
-        load_p(1)
+        load_p(4, 4)
         load_w_scales(0, (2, 3))
         load_w_words(0)
-        load_w_scales(1, (0, 1))
+        load_w_scales(1, (0, 1, 2, 3))
         load_w_words(1)
-        load_w_scales(1, (2, 3))
-        for m in range(0, M_TILES, 2):
-            nc.sync.dma_start(out=cur_sb[:, m : m + 2, :], in_=cur_view[:, m : m + 2, :])
+        load_cur(0, 1)
+        load_cur(1, 1)
+        load_cur(2, 2)
+        load_cur(4, 2)
+        load_cur(6, 2)
 
         nc.vector.tensor_scalar_max(out=upper[:], in0=avail_sb[:], scalar1=0.0)
         nc.vector.tensor_scalar(
             out=lower[:], in0=alloc_sb[:], scalar1=-1.0, scalar2=0.0, op0=ALU.mult, op1=ALU.min
         )
 
-        for a in range(HALVES):
-            for g in range(GROUPS):
-                for t in range(PACK):
-                    flipped_ps = flip.tile([P, HALF_SHOPS], BF16)
-                    for i in range(HALF_TILES):
-                        nc.tensor.transpose(
-                            out=flipped_ps[:, i * P : (i + 1) * P],
-                            in_=p_sb[:, a * HALF_TILES + i, K_PASS * g + t : K_PASS * (g + 1) : PACK],
-                            identity=identity[:],
-                        )
-                    nc.scalar.copy(out=p_flipped[:, a, g, t, :], in_=flipped_ps[:])
+        def flip(u, g):
+            flipped_ps = banks.tile([P, PACK, PAIR_SHOPS], BF16, tag="bank")
+            for t in range(PACK):
+                for i in range(PAIR_TILES):
+                    nc.tensor.transpose(
+                        out=flipped_ps[:, t, i * P : (i + 1) * P],
+                        in_=p_sb[:, u * PAIR_TILES + i, K_PASS * g + t : K_PASS * (g + 1) : PACK],
+                        identity=identity[:],
+                    )
+            nc.scalar.copy(out=p_flipped[:, u, g], in_=flipped_ps[:])
 
-        def prepare_h(a, g):
-            p_part = p_flipped[:, a, g]
-            clamped = work.tile([P, PACK, HALF_SHOPS], BF16, bufs=1)
+        def clamp(u, g):
+            clamped = work.tile([P, PACK, PAIR_SHOPS], BF16)
             for t in range(PACK):
                 column = slice(g * PACK + t, g * PACK + t + 1)
                 nc.vector.tensor_scalar(
                     out=clamped[:, t, :],
-                    in0=p_part[:, t, :],
+                    in0=p_flipped[:, u, g, t, :],
                     scalar1=lower[:, column],
                     scalar2=upper[:, column],
                     op0=ALU.max,
                     op1=ALU.min,
                 )
-            inside = work.tile([P, PACK, HALF_SHOPS], BF16, bufs=1)
-            nc.vector.tensor_tensor(out=inside[:], in0=clamped[:], in1=p_part, op=ALU.is_equal)
-            damped = work.tile([P, PACK, HALF_SHOPS], BF16)
-            nc.vector.scalar_tensor_tensor(
-                out=damped[:], in0=inside[:], scalar=DAMPING, in1=p_part, op0=ALU.max, op1=ALU.mult
+            return clamped
+
+        def mark(u, g, clamped):
+            inside = work.tile([P, PACK, PAIR_SHOPS], BF16)
+            nc.vector.tensor_tensor(
+                out=inside[:], in0=clamped[:], in1=p_flipped[:, u, g], op=ALU.is_equal
             )
-            grouped = work.tile([P, HALF_SHOPS, PACK], BF16, align_bytes=64)
+            return inside
+
+        def damp(u, g, inside):
+            damped = work.tile([P, PACK, PAIR_SHOPS], BF16)
+            nc.vector.scalar_tensor_tensor(
+                out=damped[:],
+                in0=inside[:],
+                scalar=DAMPING,
+                in1=p_flipped[:, u, g],
+                op0=ALU.max,
+                op1=ALU.mult,
+            )
+            return damped
+
+        def group(damped):
+            grouped = work.tile([P, PAIR_SHOPS, PACK], BF16, align_bytes=64)
             nc.scalar.copy(out=grouped[:], in_=damped[:].rearrange("q t s -> q s t"))
+            return grouped
+
+        def quantize(u, g, grouped):
             nc.vector.quantize_mx(
-                out=h_words[:, a, g, :].bitcast(FP8X4),
-                scales=h_planes[:, a, g, :],
+                out=h_words[:, u, g, :].bitcast(FP8X4),
+                scales=h_planes[:, u, g, :],
                 in_=grouped[:].rearrange("q s t -> q (s t)"),
             )
 
+        def prepare(u, waiting):
+            clamped = [clamp(u, g) for g in range(GROUPS)]
+            for call in waiting[:1]:
+                quantize(*call)
+            inside = [mark(u, g, clamped[g]) for g in range(GROUPS)]
+            for call in waiting[1:]:
+                quantize(*call)
+            damped = [damp(u, g, inside[g]) for g in range(GROUPS)]
+            return [(u, g, group(damped[g])) for g in range(GROUPS)]
+
         def shop_tile(m):
-            a, i = divmod(m, HALF_TILES)
+            u, i = divmod(m, PAIR_TILES)
             shops = slice(i * P, (i + 1) * P)
-            result = results.tile([P, COLS], F32)
+            result = rows.tile([P, COLS], F32, tag="row")
             for n in range(N_TILES):
                 cols = slice(n * N_TILE, (n + 1) * N_TILE)
-                j, part = divmod(n * N_TILE, PLANE_COLS)
-                acc = sums.tile([P, N_TILE], F32)
+                part, w_col = divmod(n * N_TILE, W_PART_COLS)
+                j, plane_col = divmod(n * N_TILE, PLANE_COLS)
+                acc = banks.tile([P, N_TILE], F32, tag="bank")
                 for g in range(GROUPS):
                     nc.tensor.matmul_mx(
                         out=acc[:],
-                        lhsT=h_words[:, a, g, shops].bitcast(FP8X4),
-                        lhsT_scale=h_planes[:, a, g, shops],
-                        rhs=w_words[:, g, cols].bitcast(FP8X4),
-                        rhs_scale=w_planes[4 * j : P, g, part : part + N_TILE],
+                        lhsT=h_words[:, u, g, shops].bitcast(FP8X4),
+                        lhsT_scale=h_planes[:, u, g, shops],
+                        rhs=w_words[part][:, g, w_col : w_col + N_TILE].bitcast(FP8X4),
+                        rhs_scale=w_planes[4 * j : P, g, plane_col : plane_col + N_TILE],
                         start=(g == 0),
                         stop=(g == GROUPS - 1),
                     )
@@ -173,9 +211,21 @@ def tile_optblockv2_kernel(
                 cols = slice(piece * COLS // stores, (piece + 1) * COLS // stores)
                 nc.sync.dma_start(out=out_view[:, m, cols], in_=result[:, cols])
 
+        for u in range(2):
+            for g in range(GROUPS):
+                flip(u, g)
+        waiting = prepare(0, [])
         for g in range(GROUPS):
-            prepare_h(0, g)
-        for m in range(M_TILES):
+            flip(2, g)
+        waiting = prepare(1, waiting)
+        for g in range(GROUPS):
+            flip(3, g)
+        waiting = prepare(2, waiting)
+        shop_tile(0)
+        shop_tile(1)
+        waiting = prepare(3, waiting)
+        shop_tile(2)
+        for call in waiting:
+            quantize(*call)
+        for m in range(3, M_TILES):
             shop_tile(m)
-            if m < GROUPS:
-                prepare_h(1, m)

@@ -22,12 +22,10 @@ N_TILES = COLS // N_TILE
 PAIR_TILES = 2
 PAIRS = M_TILES // PAIR_TILES
 PAIR_SHOPS = PAIR_TILES * P
-W_PARTS = 2
-W_PART_COLS = COLS // W_PARTS
 PLANE_COLS = COLS // 4
 DAMPING = 0.01
 RELIEF_EVERY = 4
-LAST_STORES = 4
+PAIR_STORES = 3
 
 FLOPS = 2 * SHOPS * BUNDLES * COLS
 
@@ -44,13 +42,11 @@ def tile_optblockv2_kernel(
     with (
         tc.tile_pool(name="keep", bufs=1) as keep,
         tc.tile_pool(name="work", bufs=2) as work,
-        tc.tile_pool(name="rows", bufs=5) as rows,
+        tc.tile_pool(name="rows", bufs=3) as rows,
         tc.psum_pool(name="banks", bufs=8) as banks,
     ):
         p_sb = rows.tile([P, M_TILES, BUNDLES], BF16, tag="row")
-        w_words_a = keep.tile([P, GROUPS, W_PART_COLS], U32, align_bytes=64)
-        w_words_b = keep.tile([P, GROUPS, W_PART_COLS], U32, align_bytes=64)
-        w_words = [w_words_a, w_words_b]
+        w_words = keep.tile([P, GROUPS, COLS], U32, align_bytes=64)
         w_planes = keep.tile([P, GROUPS, PLANE_COLS], U8, align_bytes=64)
         cur_sb = keep.tile([P, M_TILES, COLS], BF16)
         avail_sb = keep.tile([P, GROUPS * PACK], BF16)
@@ -78,9 +74,8 @@ def tile_optblockv2_kernel(
             tiles = slice(first, first + count)
             nc.sync.dma_start(out=p_sb[:, tiles, :], in_=p_view[:, tiles, :])
 
-        def load_w_words(part):
-            packed = w_view[:, :, part * W_PART_COLS * PACK : (part + 1) * W_PART_COLS * PACK]
-            nc.sync.dma_start(out=w_words[part][:].bitcast(I32), in_=packed.bitcast(I32))
+        def load_w_words(g):
+            nc.sync.dma_start(out=w_words[:, g, :].bitcast(I32), in_=w_view[:, g, :].bitcast(I32))
 
         def load_w_scales(g, quadrants):
             for quadrant in quadrants:
@@ -104,8 +99,7 @@ def tile_optblockv2_kernel(
         load_cur(0, 1)
         load_cur(1, 1)
         load_cur(2, 2)
-        load_cur(4, 2)
-        load_cur(6, 2)
+        load_cur(4, 4)
 
         nc.vector.tensor_scalar_max(out=upper[:], in0=avail_sb[:], scalar1=0.0)
         nc.vector.tensor_scalar(
@@ -178,38 +172,50 @@ def tile_optblockv2_kernel(
             damped = [damp(u, g, inside[g]) for g in range(GROUPS)]
             return [(u, g, group(damped[g])) for g in range(GROUPS)]
 
-        def shop_tile(m):
+        def multiply(m, n, g, acc):
             u, i = divmod(m, PAIR_TILES)
             shops = slice(i * P, (i + 1) * P)
-            result = rows.tile([P, COLS], F32, tag="row")
+            j, plane_col = divmod(n * N_TILE, PLANE_COLS)
+            nc.tensor.matmul_mx(
+                out=acc[:],
+                lhsT=h_words[:, u, g, shops].bitcast(FP8X4),
+                lhsT_scale=h_planes[:, u, g, shops],
+                rhs=w_words[:, g, n * N_TILE : (n + 1) * N_TILE].bitcast(FP8X4),
+                rhs_scale=w_planes[4 * j : P, g, plane_col : plane_col + N_TILE],
+                start=(g == 0),
+                stop=(g == GROUPS - 1),
+            )
+
+        def add_cur(m, n, acc, result):
+            cols = slice(n * N_TILE, (n + 1) * N_TILE)
+            part = result[:, m % PAIR_TILES, cols]
+            if n % RELIEF_EVERY == 1:
+                nc.scalar.copy(out=part, in_=acc[:])
+                nc.gpsimd.tensor_tensor(out=part, in0=part, in1=cur_sb[:, m, cols], op=ALU.add)
+            else:
+                nc.vector.tensor_tensor(out=part, in0=acc[:], in1=cur_sb[:, m, cols], op=ALU.add)
+
+        def first_shop_tile(result):
+            accs = []
             for n in range(N_TILES):
-                cols = slice(n * N_TILE, (n + 1) * N_TILE)
-                part, w_col = divmod(n * N_TILE, W_PART_COLS)
-                j, plane_col = divmod(n * N_TILE, PLANE_COLS)
+                acc = banks.tile([P, N_TILE], F32, tag="bank")
+                multiply(0, n, 0, acc)
+                accs.append(acc)
+            for n in range(N_TILES):
+                multiply(0, n, 1, accs[n])
+                add_cur(0, n, accs[n], result)
+
+        def shop_tile(m, result):
+            for n in range(N_TILES):
                 acc = banks.tile([P, N_TILE], F32, tag="bank")
                 for g in range(GROUPS):
-                    nc.tensor.matmul_mx(
-                        out=acc[:],
-                        lhsT=h_words[:, u, g, shops].bitcast(FP8X4),
-                        lhsT_scale=h_planes[:, u, g, shops],
-                        rhs=w_words[part][:, g, w_col : w_col + N_TILE].bitcast(FP8X4),
-                        rhs_scale=w_planes[4 * j : P, g, plane_col : plane_col + N_TILE],
-                        start=(g == 0),
-                        stop=(g == GROUPS - 1),
-                    )
-                if n % RELIEF_EVERY == 1:
-                    nc.scalar.copy(out=result[:, cols], in_=acc[:])
-                    nc.gpsimd.tensor_tensor(
-                        out=result[:, cols], in0=result[:, cols], in1=cur_sb[:, m, cols], op=ALU.add
-                    )
-                else:
-                    nc.vector.tensor_tensor(
-                        out=result[:, cols], in0=acc[:], in1=cur_sb[:, m, cols], op=ALU.add
-                    )
-            stores = LAST_STORES if m == M_TILES - 1 else 1
-            for piece in range(stores):
-                cols = slice(piece * COLS // stores, (piece + 1) * COLS // stores)
-                nc.sync.dma_start(out=out_view[:, m, cols], in_=result[:, cols])
+                    multiply(m, n, g, acc)
+                add_cur(m, n, acc, result)
+
+        def store(first, count, result):
+            tiles = slice(first, first + count)
+            inner = slice(first % PAIR_TILES, first % PAIR_TILES + count)
+            nc.sync.dma_start(out=out_view[:, tiles, :], in_=result[:, inner, :])
 
         for u in range(2):
             for g in range(GROUPS):
@@ -221,11 +227,20 @@ def tile_optblockv2_kernel(
         for g in range(GROUPS):
             flip(3, g)
         waiting = prepare(2, waiting)
-        shop_tile(0)
-        shop_tile(1)
-        waiting = prepare(3, waiting)
-        shop_tile(2)
-        for call in waiting:
-            quantize(*call)
-        for m in range(3, M_TILES):
-            shop_tile(m)
+        for u in range(PAIRS):
+            result = rows.tile([P, PAIR_TILES, COLS], F32, tag="row")
+            for i in range(PAIR_TILES):
+                m = u * PAIR_TILES + i
+                if m == 0:
+                    first_shop_tile(result)
+                else:
+                    shop_tile(m, result)
+                if m == 2:
+                    for call in waiting:
+                        quantize(*call)
+                if u >= PAIR_STORES:
+                    store(m, 1, result)
+            if u < PAIR_STORES:
+                store(u * PAIR_TILES, PAIR_TILES, result)
+            if u == 0:
+                waiting = prepare(3, waiting)

@@ -25,7 +25,7 @@ PAIR_SHOPS = PAIR_TILES * P
 PLANE_COLS = COLS // 4
 DAMPING = 0.01
 RELIEF_EVERY = 4
-PAIR_STORES = 3
+PAIR_STORES = 2
 
 FLOPS = 2 * SHOPS * BUNDLES * COLS
 

@@ -49,8 +49,7 @@ def tile_optblockv2_kernel(
         w_words = keep.tile([P, GROUPS, COLS], U32, align_bytes=64)
         w_planes = keep.tile([P, GROUPS, PLANE_COLS], U8, align_bytes=64)
         cur_sb = keep.tile([P, M_TILES, COLS], BF16)
-        avail_sb = keep.tile([P, GROUPS * PACK], BF16)
-        alloc_sb = keep.tile([P, GROUPS * PACK], BF16)
+        bound_rows = keep.tile([P, BUNDLES], BF16)
         upper = keep.tile([P, GROUPS * PACK], F32)
         lower = keep.tile([P, GROUPS * PACK], F32)
         identity = keep.tile([P, P], BF16)
@@ -58,17 +57,15 @@ def tile_optblockv2_kernel(
         h_words = keep.tile([P, PAIRS, GROUPS, PAIR_SHOPS], U32, align_bytes=64)
         h_planes = keep.tile([P, PAIRS, GROUPS, PAIR_SHOPS], U8, align_bytes=64)
 
+        nc.vector.memset(bound_rows[:].bitcast(I32), 0)
         nc.vector.memset(w_planes[:].bitcast(I32), 0)
         make_identity(nc, identity[:])
 
-        nc.scalar.dma_start(
-            out=avail_sb[:].rearrange("q (g t) -> q g t", t=PACK),
-            in_=avail_bundle.rearrange("(g q t) -> q g t", g=GROUPS, t=PACK),
-        )
-        nc.scalar.dma_start(
-            out=alloc_sb[:].rearrange("q (g t) -> q g t", t=PACK),
-            in_=alloc_bundle.rearrange("(g q t) -> q g t", g=GROUPS, t=PACK),
-        )
+        for row, bundle_bound in enumerate((avail_bundle, alloc_bundle)):
+            nc.scalar.dma_start(
+                out=bound_rows[row : row + 1, :],
+                in_=bundle_bound.rearrange("(o k) -> o k", o=1),
+            )
 
         def load_p(first, count):
             tiles = slice(first, first + count)
@@ -96,15 +93,28 @@ def tile_optblockv2_kernel(
         load_w_words(0)
         load_w_scales(1, (0, 1, 2, 3))
         load_w_words(1)
-        load_cur(0, 1)
-        load_cur(1, 1)
+        load_cur(0, 2)
         load_cur(2, 2)
         load_cur(4, 4)
 
-        nc.vector.tensor_scalar_max(out=upper[:], in0=avail_sb[:], scalar1=0.0)
-        nc.vector.tensor_scalar(
-            out=lower[:], in0=alloc_sb[:], scalar1=-1.0, scalar2=0.0, op0=ALU.mult, op1=ALU.min
-        )
+        def flip_bounds():
+            bounds_ps = banks.tile([P, GROUPS * PACK, P], BF16, tag="bank")
+            for g in range(GROUPS):
+                for t in range(PACK):
+                    nc.tensor.transpose(
+                        out=bounds_ps[:, g * PACK + t, :],
+                        in_=bound_rows[:, K_PASS * g + t : K_PASS * (g + 1) : PACK],
+                        identity=identity[:],
+                    )
+            nc.vector.tensor_scalar_max(out=upper[:], in0=bounds_ps[:, :, 0], scalar1=0.0)
+            nc.vector.tensor_scalar(
+                out=lower[:],
+                in0=bounds_ps[:, :, 1],
+                scalar1=-1.0,
+                scalar2=0.0,
+                op0=ALU.mult,
+                op1=ALU.min,
+            )
 
         def flip(u, g):
             flipped_ps = banks.tile([P, PACK, PAIR_SHOPS], BF16, tag="bank")
@@ -217,9 +227,11 @@ def tile_optblockv2_kernel(
             inner = slice(first % PAIR_TILES, first % PAIR_TILES + count)
             nc.sync.dma_start(out=out_view[:, tiles, :], in_=result[:, inner, :])
 
-        for u in range(2):
-            for g in range(GROUPS):
-                flip(u, g)
+        for g in range(GROUPS):
+            flip(0, g)
+        flip_bounds()
+        for g in range(GROUPS):
+            flip(1, g)
         waiting = prepare(0, [])
         for g in range(GROUPS):
             flip(2, g)

@@ -19,12 +19,14 @@ GROUPS = BUNDLES // K_PASS
 M_TILES = SHOPS // P
 N_TILE = 512
 N_TILES = COLS // N_TILE
+WARM_AHEAD = 6
+WARM_BEHIND = 8
 PAIR_TILES = 2
 PAIRS = M_TILES // PAIR_TILES
 PAIR_SHOPS = PAIR_TILES * P
 PLANE_COLS = COLS // 4
 DAMPING = 0.01
-RELIEF_EVERY = 4
+RELIEF_EVERY = 3
 PAIR_STORES = 2
 
 FLOPS = 2 * SHOPS * BUNDLES * COLS
@@ -50,13 +52,15 @@ def tile_optblockv2_kernel(
         w_planes = keep.tile([P, GROUPS, PLANE_COLS], U8, align_bytes=64)
         cur_sb = keep.tile([P, M_TILES, COLS], BF16)
         bound_rows = keep.tile([P, BUNDLES], BF16)
+        zeros = keep.tile([P, N_TILE], BF16)
         upper = keep.tile([P, GROUPS * PACK], F32)
         lower = keep.tile([P, GROUPS * PACK], F32)
         identity = keep.tile([P, P], BF16)
-        p_flipped = keep.tile([P, PAIRS, GROUPS, PACK, PAIR_SHOPS], BF16)
+        p_flipped = keep.tile([P, GROUPS, PACK, PAIR_SHOPS], BF16)
         h_words = keep.tile([P, PAIRS, GROUPS, PAIR_SHOPS], U32, align_bytes=64)
         h_planes = keep.tile([P, PAIRS, GROUPS, PAIR_SHOPS], U8, align_bytes=64)
 
+        nc.vector.memset(zeros[:].bitcast(I32), 0)
         nc.vector.memset(bound_rows[:].bitcast(I32), 0)
         nc.vector.memset(w_planes[:].bitcast(I32), 0)
         make_identity(nc, identity[:])
@@ -87,13 +91,13 @@ def tile_optblockv2_kernel(
             nc.sync.dma_start(out=cur_sb[:, tiles, :], in_=cur_view[:, tiles, :])
 
         load_p(0, 4)
-        load_w_scales(0, (0, 1))
-        load_p(4, 4)
-        load_w_scales(0, (2, 3))
+        load_w_scales(0, (0, 1, 2, 3))
         load_w_words(0)
         load_w_scales(1, (0, 1, 2, 3))
         load_w_words(1)
-        load_cur(0, 2)
+        load_cur(0, 1)
+        load_cur(1, 1)
+        load_p(4, 4)
         load_cur(2, 2)
         load_cur(4, 4)
 
@@ -125,15 +129,20 @@ def tile_optblockv2_kernel(
                         in_=p_sb[:, u * PAIR_TILES + i, K_PASS * g + t : K_PASS * (g + 1) : PACK],
                         identity=identity[:],
                     )
-            nc.scalar.copy(out=p_flipped[:, u, g], in_=flipped_ps[:])
+            return flipped_ps[:]
 
-        def clamp(u, g):
+        def flip_to_sbuf(u, g):
+            flipped_ps = flip(u, g)
+            nc.scalar.copy(out=p_flipped[:, g], in_=flipped_ps)
+            return p_flipped[:, g]
+
+        def clamp(g, flipped):
             clamped = work.tile([P, PACK, PAIR_SHOPS], BF16)
             for t in range(PACK):
                 column = slice(g * PACK + t, g * PACK + t + 1)
                 nc.vector.tensor_scalar(
                     out=clamped[:, t, :],
-                    in0=p_flipped[:, u, g, t, :],
+                    in0=flipped[:, t, :],
                     scalar1=lower[:, column],
                     scalar2=upper[:, column],
                     op0=ALU.max,
@@ -141,27 +150,23 @@ def tile_optblockv2_kernel(
                 )
             return clamped
 
-        def mark(u, g, clamped):
+        def mark(flipped, clamped):
             inside = work.tile([P, PACK, PAIR_SHOPS], BF16)
-            nc.vector.tensor_tensor(
-                out=inside[:], in0=clamped[:], in1=p_flipped[:, u, g], op=ALU.is_equal
-            )
+            nc.vector.tensor_tensor(out=inside[:], in0=clamped[:], in1=flipped, op=ALU.is_equal)
             return inside
 
-        def damp(u, g, inside):
-            damped = work.tile([P, PACK, PAIR_SHOPS], BF16)
+        def damp_into(damped, flipped, inside):
             nc.vector.scalar_tensor_tensor(
-                out=damped[:],
-                in0=inside[:],
-                scalar=DAMPING,
-                in1=p_flipped[:, u, g],
-                op0=ALU.max,
-                op1=ALU.mult,
+                out=damped, in0=inside, scalar=DAMPING, in1=flipped, op0=ALU.max, op1=ALU.mult
             )
+
+        def damp(flipped, inside):
+            damped = work.tile([P, PACK, PAIR_SHOPS], BF16)
+            damp_into(damped[:], flipped, inside[:])
             return damped
 
         def group(damped):
-            grouped = work.tile([P, PAIR_SHOPS, PACK], BF16, align_bytes=64)
+            grouped = work.tile([P, PAIR_SHOPS, PACK], BF16, align_bytes=64, tag="grouped")
             nc.scalar.copy(out=grouped[:], in_=damped[:].rearrange("q t s -> q s t"))
             return grouped
 
@@ -172,14 +177,29 @@ def tile_optblockv2_kernel(
                 in_=grouped[:].rearrange("q s t -> q (s t)"),
             )
 
-        def prepare(u, waiting):
-            clamped = [clamp(u, g) for g in range(GROUPS)]
+        def prepare_first(flipped):
+            clamped = [clamp(g, flipped[g]) for g in range(GROUPS)]
+            inside = [mark(flipped[g], clamped[g]) for g in range(GROUPS)]
+            grouped = []
+            for g in range(GROUPS):
+                damped = work.tile([P, PAIR_SHOPS, PACK], BF16, align_bytes=64, tag="grouped", name="damped_first")
+                damp_into(
+                    damped[:],
+                    flipped[g].rearrange("q t s -> q s t"),
+                    inside[g][:].rearrange("q t s -> q s t"),
+                )
+                grouped.append(damped)
+            for g in range(GROUPS):
+                quantize(0, g, grouped[g])
+
+        def prepare(u, flipped, waiting):
+            clamped = [clamp(g, flipped[g]) for g in range(GROUPS)]
             for call in waiting[:1]:
                 quantize(*call)
-            inside = [mark(u, g, clamped[g]) for g in range(GROUPS)]
+            inside = [mark(flipped[g], clamped[g]) for g in range(GROUPS)]
             for call in waiting[1:]:
                 quantize(*call)
-            damped = [damp(u, g, inside[g]) for g in range(GROUPS)]
+            damped = [damp(flipped[g], inside[g]) for g in range(GROUPS)]
             return [(u, g, group(damped[g])) for g in range(GROUPS)]
 
         def multiply(m, n, g, acc):
@@ -199,7 +219,7 @@ def tile_optblockv2_kernel(
         def add_cur(m, n, acc, result):
             cols = slice(n * N_TILE, (n + 1) * N_TILE)
             part = result[:, m % PAIR_TILES, cols]
-            if n % RELIEF_EVERY == 1:
+            if n % RELIEF_EVERY == 0:
                 nc.scalar.copy(out=part, in_=acc[:])
                 nc.gpsimd.tensor_tensor(out=part, in0=part, in1=cur_sb[:, m, cols], op=ALU.add)
             else:
@@ -227,18 +247,28 @@ def tile_optblockv2_kernel(
             inner = slice(first % PAIR_TILES, first % PAIR_TILES + count)
             nc.sync.dma_start(out=out_view[:, tiles, :], in_=result[:, inner, :])
 
-        for g in range(GROUPS):
-            flip(0, g)
-        flip_bounds()
-        for g in range(GROUPS):
-            flip(1, g)
-        waiting = prepare(0, [])
-        for g in range(GROUPS):
-            flip(2, g)
-        waiting = prepare(1, waiting)
-        for g in range(GROUPS):
-            flip(3, g)
-        waiting = prepare(2, waiting)
+        spare = banks.tile([P, N_TILE], F32, tag="bank")
+
+        def keep_warm(count):
+            for call in range(count):
+                nc.tensor.matmul(
+                    out=spare[:], lhsT=zeros[:, :P], rhs=zeros[:], start=True, stop=True
+                )
+
+        flipped = []
+        flipped_next = []
+        with tc.manual_schedule(engines={mybir.EngineType.PE}):
+            keep_warm(WARM_AHEAD)
+            flip_bounds()
+            for g in range(GROUPS):
+                flipped.append(flip(0, g))
+                keep_warm(1)
+            for g in range(GROUPS):
+                flipped_next.append(flip_to_sbuf(1, g))
+                keep_warm(1)
+            keep_warm(WARM_BEHIND)
+        prepare_first(flipped)
+        waiting = prepare(1, flipped_next, [])
         for u in range(PAIRS):
             result = rows.tile([P, PAIR_TILES, COLS], F32, tag="row")
             for i in range(PAIR_TILES):
@@ -247,12 +277,15 @@ def tile_optblockv2_kernel(
                     first_shop_tile(result)
                 else:
                     shop_tile(m, result)
-                if m == 2:
+                if i == 0:
                     for call in waiting:
                         quantize(*call)
                 if u >= PAIR_STORES:
                     store(m, 1, result)
             if u < PAIR_STORES:
                 store(u * PAIR_TILES, PAIR_TILES, result)
-            if u == 0:
-                waiting = prepare(3, waiting)
+            later = u + 2
+            waiting = []
+            if later < PAIRS:
+                flipped = [flip(later, g) for g in range(GROUPS)]
+                waiting = prepare(later, flipped, [])

@@ -19,6 +19,7 @@ GROUPS = BUNDLES // K_PASS
 M_TILES = SHOPS // P
 N_TILE = 512
 N_TILES = COLS // N_TILE
+BOUND_GAP = 32
 WARM_AHEAD = 6
 WARM_BEHIND = 8
 PAIR_TILES = 2
@@ -51,7 +52,7 @@ def tile_optblockv2_kernel(
         w_words = keep.tile([P, GROUPS, COLS], U32, align_bytes=64)
         w_planes = keep.tile([P, GROUPS, PLANE_COLS], U8, align_bytes=64)
         cur_sb = keep.tile([P, M_TILES, COLS], BF16)
-        bound_rows = keep.tile([P, BUNDLES], BF16)
+        bound_rows = keep.tile([P, GROUPS, K_PASS + BOUND_GAP], BF16)
         zeros = keep.tile([P, N_TILE], BF16)
         upper = keep.tile([P, GROUPS * PACK], F32)
         lower = keep.tile([P, GROUPS * PACK], F32)
@@ -61,14 +62,14 @@ def tile_optblockv2_kernel(
         h_planes = keep.tile([P, PAIRS, GROUPS, PAIR_SHOPS], U8, align_bytes=64)
 
         nc.vector.memset(zeros[:].bitcast(I32), 0)
-        nc.vector.memset(bound_rows[:].bitcast(I32), 0)
+        nc.vector.memset(bound_rows[:].rearrange("q g k -> q (g k)").bitcast(I32), 0)
         nc.vector.memset(w_planes[:].bitcast(I32), 0)
         make_identity(nc, identity[:])
 
         for row, bundle_bound in enumerate((avail_bundle, alloc_bundle)):
             nc.scalar.dma_start(
-                out=bound_rows[row : row + 1, :],
-                in_=bundle_bound.rearrange("(o k) -> o k", o=1),
+                out=bound_rows[row : row + 1, :, :K_PASS],
+                in_=bundle_bound.rearrange("(o g k) -> o g k", o=1, g=GROUPS),
             )
 
         def load_p(first, count):
@@ -107,7 +108,7 @@ def tile_optblockv2_kernel(
                 for t in range(PACK):
                     nc.tensor.transpose(
                         out=bounds_ps[:, g * PACK + t, :],
-                        in_=bound_rows[:, K_PASS * g + t : K_PASS * (g + 1) : PACK],
+                        in_=bound_rows[:, g, t:K_PASS:PACK],
                         identity=identity[:],
                     )
             nc.vector.tensor_scalar_max(out=upper[:], in0=bounds_ps[:, :, 0], scalar1=0.0)

import concourse.mybir as mybir
from concourse.masks import make_identity

F32 = mybir.dt.float32
BF16 = mybir.dt.bfloat16
I32 = mybir.dt.int32
U32 = mybir.dt.uint32
U8 = mybir.dt.uint8
FP8X4 = mybir.dt.float8_e4m3fn_x4
ALU = mybir.AluOpType

P = 128
PACK = 4
K_PASS = P * PACK
SHOPS = 1024
BUNDLES = 1024
COLS = 4096
GROUPS = BUNDLES // K_PASS
M_TILES = SHOPS // P
N_TILE = 512
N_TILES = COLS // N_TILE
BOUND_GAP = 32
WARM_AHEAD = 6
WARM_BEHIND = 8
PAIR_TILES = 2
PAIRS = M_TILES // PAIR_TILES
PAIR_SHOPS = PAIR_TILES * P
PLANE_COLS = COLS // 4
DAMPING = 0.01
RELIEF_EVERY = 3
PAIR_STORES = 2

FLOPS = 2 * SHOPS * BUNDLES * COLS


def tile_optblockv2_kernel(
    tc, proba, cur_inven, bun_sc_words, bun_sc_scales, avail_bundle, alloc_bundle, out
):
    nc = tc.nc
    p_view = proba.rearrange("(r m k) -> r m k", m=M_TILES, k=BUNDLES)
    cur_view = cur_inven.rearrange("(r m) n -> r m n", m=M_TILES)
    out_view = out.rearrange("o (r m n) -> (o r) m n", m=M_TILES, n=COLS)
    w_view = bun_sc_words.rearrange("g q n t -> q g (n t)")

    with (
        tc.tile_pool(name="keep", bufs=1) as keep,
        tc.tile_pool(name="work", bufs=2) as work,
        tc.tile_pool(name="rows", bufs=3) as rows,
        tc.psum_pool(name="banks", bufs=8) as banks,
    ):
        p_sb = rows.tile([P, M_TILES, BUNDLES], BF16, tag="row")
        w_words = keep.tile([P, GROUPS, COLS], U32, align_bytes=64)
        w_planes = keep.tile([P, GROUPS, PLANE_COLS], U8, align_bytes=64)
        cur_sb = keep.tile([P, M_TILES, COLS], BF16)
        bound_rows = keep.tile([P, GROUPS, K_PASS + BOUND_GAP], BF16)
        zeros = keep.tile([P, N_TILE], BF16)
        upper = keep.tile([P, GROUPS * PACK], F32)
        lower = keep.tile([P, GROUPS * PACK], F32)
        identity = keep.tile([P, P], BF16)
        p_flipped = keep.tile([P, GROUPS, PACK, PAIR_SHOPS], BF16)
        h_words = keep.tile([P, PAIRS, GROUPS, PAIR_SHOPS], U32, align_bytes=64)
        h_planes = keep.tile([P, PAIRS, GROUPS, PAIR_SHOPS], U8, align_bytes=64)

        nc.vector.memset(zeros[:].bitcast(I32), 0)
        nc.vector.memset(bound_rows[:].rearrange("q g k -> q (g k)").bitcast(I32), 0)
        nc.vector.memset(w_planes[:].bitcast(I32), 0)
        make_identity(nc, identity[:])

        for row, bundle_bound in enumerate((avail_bundle, alloc_bundle)):
            nc.scalar.dma_start(
                out=bound_rows[row : row + 1, :, :K_PASS],
                in_=bundle_bound.rearrange("(o g k) -> o g k", o=1, g=GROUPS),
            )

        def load_p(first, count):
            tiles = slice(first, first + count)
            nc.sync.dma_start(out=p_sb[:, tiles, :], in_=p_view[:, tiles, :])

        def load_w_words(g):
            nc.sync.dma_start(out=w_words[:, g, :].bitcast(I32), in_=w_view[:, g, :].bitcast(I32))

        def load_w_scales(g, quadrants):
            for quadrant in quadrants:
                scale_rows = bun_sc_scales[g, 4 * quadrant : 4 * quadrant + 4, :].bitcast(I32)
                nc.sync.dma_start(
                    out=w_planes[32 * quadrant : 32 * quadrant + 16, g, :].bitcast(I32),
                    in_=scale_rows.rearrange("r (j n) -> j r n", j=4),
                )

        def load_cur(first, count):
            tiles = slice(first, first + count)
            nc.sync.dma_start(out=cur_sb[:, tiles, :], in_=cur_view[:, tiles, :])

        load_p(0, 4)
        load_w_scales(0, (0, 1, 2, 3))
        load_w_words(0)
        load_w_scales(1, (0, 1, 2, 3))
        load_w_words(1)
        load_cur(0, 1)
        load_cur(1, 1)
        load_p(4, 4)
        load_cur(2, 2)
        load_cur(4, 4)

        def flip_bounds():
            bounds_ps = banks.tile([P, GROUPS * PACK, P], BF16, tag="bank")
            for g in range(GROUPS):
                for t in range(PACK):
                    nc.tensor.transpose(
                        out=bounds_ps[:, g * PACK + t, :],
                        in_=bound_rows[:, g, t:K_PASS:PACK],
                        identity=identity[:],
                    )
            nc.vector.tensor_scalar_max(out=upper[:], in0=bounds_ps[:, :, 0], scalar1=0.0)
            nc.vector.tensor_scalar(
                out=lower[:],
                in0=bounds_ps[:, :, 1],
                scalar1=-1.0,
                scalar2=0.0,
                op0=ALU.mult,
                op1=ALU.min,
            )

        def flip(u, g):
            flipped_ps = banks.tile([P, PACK, PAIR_SHOPS], BF16, tag="bank")
            for t in range(PACK):
                for i in range(PAIR_TILES):
                    nc.tensor.transpose(
                        out=flipped_ps[:, t, i * P : (i + 1) * P],
                        in_=p_sb[:, u * PAIR_TILES + i, K_PASS * g + t : K_PASS * (g + 1) : PACK],
                        identity=identity[:],
                    )
            return flipped_ps[:]

        def flip_to_sbuf(u, g):
            flipped_ps = flip(u, g)
            nc.scalar.copy(out=p_flipped[:, g], in_=flipped_ps)
            return p_flipped[:, g]

        def clamp(g, flipped):
            clamped = work.tile([P, PACK, PAIR_SHOPS], BF16)
            for t in range(PACK):
                column = slice(g * PACK + t, g * PACK + t + 1)
                nc.vector.tensor_scalar(
                    out=clamped[:, t, :],
                    in0=flipped[:, t, :],
                    scalar1=lower[:, column],
                    scalar2=upper[:, column],
                    op0=ALU.max,
                    op1=ALU.min,
                )
            return clamped

        def mark(flipped, clamped):
            inside = work.tile([P, PACK, PAIR_SHOPS], BF16)
            nc.vector.tensor_tensor(out=inside[:], in0=clamped[:], in1=flipped, op=ALU.is_equal)
            return inside

        def damp_into(damped, flipped, inside):
            nc.vector.scalar_tensor_tensor(
                out=damped, in0=inside, scalar=DAMPING, in1=flipped, op0=ALU.max, op1=ALU.mult
            )

        def damp(flipped, inside):
            damped = work.tile([P, PACK, PAIR_SHOPS], BF16)
            damp_into(damped[:], flipped, inside[:])
            return damped

        def group(damped):
            grouped = work.tile([P, PAIR_SHOPS, PACK], BF16, align_bytes=64, tag="grouped")
            nc.scalar.copy(out=grouped[:], in_=damped[:].rearrange("q t s -> q s t"))
            return grouped

        def quantize(u, g, grouped):
            nc.vector.quantize_mx(
                out=h_words[:, u, g, :].bitcast(FP8X4),
                scales=h_planes[:, u, g, :],
                in_=grouped[:].rearrange("q s t -> q (s t)"),
            )

        def prepare_first(flipped):
            clamped = [clamp(g, flipped[g]) for g in range(GROUPS)]
            inside = [mark(flipped[g], clamped[g]) for g in range(GROUPS)]
            grouped = []
            for g in range(GROUPS):
                damped = work.tile([P, PAIR_SHOPS, PACK], BF16, align_bytes=64, tag="grouped", name="damped_first")
                damp_into(
                    damped[:],
                    flipped[g].rearrange("q t s -> q s t"),
                    inside[g][:].rearrange("q t s -> q s t"),
                )
                grouped.append(damped)
            for g in range(GROUPS):
                quantize(0, g, grouped[g])

        def prepare(u, flipped, waiting):
            clamped = [clamp(g, flipped[g]) for g in range(GROUPS)]
            for call in waiting[:1]:
                quantize(*call)
            inside = [mark(flipped[g], clamped[g]) for g in range(GROUPS)]
            for call in waiting[1:]:
                quantize(*call)
            damped = [damp(flipped[g], inside[g]) for g in range(GROUPS)]
            return [(u, g, group(damped[g])) for g in range(GROUPS)]

        def multiply(m, n, g, acc):
            u, i = divmod(m, PAIR_TILES)
            shops = slice(i * P, (i + 1) * P)
            j, plane_col = divmod(n * N_TILE, PLANE_COLS)
            nc.tensor.matmul_mx(
                out=acc[:],
                lhsT=h_words[:, u, g, shops].bitcast(FP8X4),
                lhsT_scale=h_planes[:, u, g, shops],
                rhs=w_words[:, g, n * N_TILE : (n + 1) * N_TILE].bitcast(FP8X4),
                rhs_scale=w_planes[4 * j : P, g, plane_col : plane_col + N_TILE],
                start=(g == 0),
                stop=(g == GROUPS - 1),
            )

        def add_cur(m, n, acc, result):
            cols = slice(n * N_TILE, (n + 1) * N_TILE)
            part = result[:, m % PAIR_TILES, cols]
            if n % RELIEF_EVERY == 0:
                nc.scalar.copy(out=part, in_=acc[:])
                nc.gpsimd.tensor_tensor(out=part, in0=part, in1=cur_sb[:, m, cols], op=ALU.add)
            else:
                nc.vector.tensor_tensor(out=part, in0=acc[:], in1=cur_sb[:, m, cols], op=ALU.add)

        def first_shop_tile(result):
            accs = []
            for n in range(N_TILES):
                acc = banks.tile([P, N_TILE], F32, tag="bank")
                multiply(0, n, 0, acc)
                accs.append(acc)
            for n in range(N_TILES):
                multiply(0, n, 1, accs[n])
                add_cur(0, n, accs[n], result)

        def shop_tile(m, result):
            for n in range(N_TILES):
                acc = banks.tile([P, N_TILE], F32, tag="bank")
                for g in range(GROUPS):
                    multiply(m, n, g, acc)
                add_cur(m, n, acc, result)

        def store(first, count, result):
            tiles = slice(first, first + count)
            inner = slice(first % PAIR_TILES, first % PAIR_TILES + count)
            nc.sync.dma_start(out=out_view[:, tiles, :], in_=result[:, inner, :])

        spare = banks.tile([P, N_TILE], F32, tag="bank")

        def keep_warm(count):
            for call in range(count):
                nc.tensor.matmul(
                    out=spare[:], lhsT=zeros[:, :P], rhs=zeros[:], start=True, stop=True
                )

        flipped = []
        flipped_next = []
        with tc.manual_schedule(engines={mybir.EngineType.PE}):
            keep_warm(WARM_AHEAD)
            flip_bounds()
            for g in range(GROUPS):
                flipped.append(flip(0, g))
                keep_warm(1)
            for g in range(GROUPS):
                flipped_next.append(flip_to_sbuf(1, g))
                keep_warm(1)
            keep_warm(WARM_BEHIND)
        prepare_first(flipped)
        waiting = prepare(1, flipped_next, [])
        for u in range(PAIRS):
            result = rows.tile([P, PAIR_TILES, COLS], F32, tag="row")
            for i in range(PAIR_TILES):
                m = u * PAIR_TILES + i
                if m == 0:
                    first_shop_tile(result)
                else:
                    shop_tile(m, result)
                if i == 0:
                    for call in waiting:
                        quantize(*call)
                if u >= PAIR_STORES:
                    store(m, 1, result)
            if u < PAIR_STORES:
                store(u * PAIR_TILES, PAIR_TILES, result)
            later = u + 2
            waiting = []
            if later < PAIRS:
                flipped = [flip(later, g) for g in range(GROUPS)]
                waiting = prepare(later, flipped, [])
